import numpy as np
import ml_dtypes


def mxq(x, axis, fmt="e4m3"):
    dtype, down = {"e4m3": (ml_dtypes.float8_e4m3fn, 7), "e5m2": (ml_dtypes.float8_e5m2, 14)}[fmt]
    v = np.moveaxis(np.asarray(x, np.float32).astype(ml_dtypes.bfloat16).astype(np.float64), axis, -1)
    blocks = v.reshape(v.shape[:-1] + (-1, 32))
    amax = np.abs(blocks).max(-1, keepdims=True)
    byte = np.maximum(np.where(amax > 0, np.frexp(amax)[1] - 1 + 127, 0) - down, 1)
    scale = np.exp2(byte - 127.0)
    codes = (blocks / scale).astype(np.float32).astype(dtype).astype(np.float64)
    return np.moveaxis((codes * scale).reshape(v.shape), -1, axis)


WIDE = False


def mx_kscale(k):
    if not WIDE:
        return np.ones(k)
    levels = np.array([10, -10, 5, -5, 0])
    if k % 512:
        return np.exp2(np.random.permutation(np.resize(levels, k // 32))).repeat(32)
    a = np.empty((k // 512, 16))
    for p in range(k // 512):
        a[p, :8] = np.random.permutation(np.resize(levels, 8))
        for g in range(8):
            far = levels[np.abs(levels - a[p, g]) >= 10]
            a[p, g + 8] = far[np.random.randint(len(far))]
    return np.exp2(a.ravel()).repeat(32)


BF16 = ml_dtypes.bfloat16


def bf(x):
    return np.asarray(x, np.float32).astype(BF16)


def f64(x):
    return np.asarray(x).astype(np.float64)


E2M1 = np.array([0.0, 0.5, 1.0, 1.5, 2.0, 3.0, 4.0, 6.0, -0.0, -0.5, -1.0, -1.5, -2.0, -3.0, -4.0, -6.0])


def pack_weight(w, fmt):
    k, n = w.shape
    w = f64(bf(w)).reshape(k // 32, 32, n)
    amax = np.abs(w).max(1)
    if fmt == "e4m3":
        byte = np.frexp(amax)[1] - 1 + 127 - 7
    else:
        mant, ex = np.frexp(amax / 6.0)
        byte = np.where(mant > 0.5, ex, ex - 1) + 127
    byte = np.clip(np.where(amax > 0, byte, 1), 1, 254)
    scaled = (w * np.exp2(127.0 - byte)[:, None, :]).reshape(k, n).astype(np.float32)
    by_word = np.ascontiguousarray(scaled.reshape(k // 512, 128, 4, n).transpose(0, 1, 3, 2))
    if fmt == "e4m3":
        words = by_word.astype(ml_dtypes.float8_e4m3fn).view(np.uint8)
    else:
        c = by_word.astype(ml_dtypes.float4_e2m1fn).view(np.uint8) & 0xF
        words = c[..., 0::2] | (c[..., 1::2] << 4)
    return np.ascontiguousarray(words), np.ascontiguousarray(byte.astype(np.uint8).reshape(k // 512, 16, n))


def unpack_weight(words, scales, fmt):
    g, p, n, _ = words.shape
    if fmt == "e4m3":
        vals = np.ascontiguousarray(words).view(ml_dtypes.float8_e4m3fn).astype(np.float64)
    else:
        nib = np.empty((g, p, n, 4), np.uint8)
        nib[..., 0::2] = words & 0xF
        nib[..., 1::2] = words >> 4
        vals = E2M1[nib]
    vals = vals * np.repeat(np.exp2(scales.astype(np.float64) - 127.0), 8, axis=1)[..., None]
    return vals.transpose(0, 1, 3, 2).reshape(g * 512, n)
def pack4(w):
    words, scales = pack_weight(w, "e2m1")
    return words.reshape(words.shape[0], 128, -1), scales


def unpack4(words, scales):
    return unpack_weight(words.reshape(words.shape[0], 128, -1, 2), scales, "e2m1")


B, S, H, HD = 4, 2048, 4, 128
DIM = H * HD


def draw0():
    s, t = mx_kscale(DIM), mx_kscale(DIM)
    x = bf(np.random.standard_normal((B, S, DIM)) * 2.0 * s)
    y_norm = bf(np.random.standard_normal((B, S, DIM)))
    wg_w_words, wg_w_scales = pack4(np.random.standard_normal((DIM, DIM)) * 0.5 / np.sqrt(DIM) / s[:, None] * t)
    wo_w_words, wo_w_scales = pack4(np.random.standard_normal((DIM, DIM)) * 1.5 / np.sqrt(DIM) / t[:, None])
    return {"x": x,
            "y_norm": y_norm,
            "wg_w_words": wg_w_words, "wg_w_scales": wg_w_scales,
            "wo_w_words": wo_w_words, "wo_w_scales": wo_w_scales}


def core(x, y_norm, wg_w_words, wg_w_scales, wo_w_words, wo_w_scales):
    g = np.maximum(mxq(f64(x), 2, "e4m3") @ unpack4(wg_w_words, wg_w_scales), 0.0)
    h = g * f64(y_norm)
    return mxq(h, 2, "e4m3") @ unpack4(wo_w_words, wo_w_scales)


def e4m3fn_bytes(y):
    return np.clip(np.asarray(y, np.float64), -448.0, 448.0).astype(np.float32).astype(ml_dtypes.float8_e4m3fn).view(np.uint8)


def e4m3fn_values(b):
    return np.asarray(b, np.uint8).view(ml_dtypes.float8_e4m3fn).astype(np.float64)


def setup_inputs():
    d = draw0()
    x0 = np.asarray(d['x']).astype(np.float64)
    s = (np.max(np.abs(x0), axis=(0, 1), keepdims=True) / 448.0).astype(np.float32)
    out = {}
    for k, v in d.items():
        if k == 'x':
            out['x_bytes'] = e4m3fn_bytes(x0 / s.astype(np.float64))
            out['x_scale'] = s
        else:
            out[k] = v
    return out


def reference(x_bytes, x_scale, y_norm, wg_w_words, wg_w_scales, wo_w_words, wo_w_scales):
    return core(e4m3fn_values(x_bytes) * x_scale.astype(np.float64), y_norm, wg_w_words, wg_w_scales, wo_w_words, wo_w_scales)

@@ -1,0 +1,198 @@
+from contextlib import ExitStack
+
+import concourse.mybir as mybir
+from concourse.masks import make_identity
+
+F32 = mybir.dt.float32
+BF16 = mybir.dt.bfloat16
+I32 = mybir.dt.int32
+U32 = mybir.dt.uint32
+U8 = mybir.dt.uint8
+FP8 = mybir.dt.float8_e4m3fn
+FP8X4 = mybir.dt.float8_e4m3fn_x4
+FP4X4 = mybir.dt.float4_e2m1fn_x4
+ALU = mybir.AluOpType
+
+P = 128
+TOKENS = 8192
+DIM = 512
+FLOPS = 2 * 2 * TOKENS * DIM * DIM
+
+ROWS = TOKENS // P
+PAIRS = ROWS // 2
+AHEAD = 8
+LEAD = 4
+SHARE = 384
+HINGE = 16
+
+
+def load_weight(nc, keep, words, scales, name):
+    w = keep.tile([P, 2 * DIM], U8, name=name + "_codes", align_bytes=64)
+    s = keep.tile([P, DIM], U8, name=name + "_scales", align_bytes=64)
+    nc.vector.memset(s[:].bitcast(I32), 0)
+    nc.sync.dma_start(out=w[:], in_=words[0])
+    for q in range(4):
+        nc.sync.dma_start(
+            out=s[32 * q : 32 * q + 4, :].bitcast(I32),
+            in_=scales[0][4 * q : 4 * q + 4, :].bitcast(I32),
+        )
+    return w, s
+
+
+def tile_multiscaleretention_pb_t_w4_kernel(
+    tc, x_bytes, x_scale, y_norm, wg_words, wg_scales, wo_words, wo_scales, out
+):
+    nc = tc.nc
+    x_rows = x_bytes.rearrange("b s k -> (b s) k").rearrange("(p r) k -> p r k", p=P)
+    y_rows = y_norm.rearrange("b s k -> (b s) k").rearrange("(p r) k -> p r k", p=P)
+    o_rows = out.rearrange("b s k -> (b s) k").rearrange("(p r) k -> p r k", p=P)
+
+    with ExitStack() as ctx:
+        keep = ctx.enter_context(tc.tile_pool(name="keep", bufs=1))
+        pool = ctx.enter_context(tc.tile_pool(name="pool", bufs=3))
+        outs = ctx.enter_context(tc.tile_pool(name="outs", bufs=4))
+        psum = ctx.enter_context(tc.psum_pool(name="psum", bufs=2))
+
+        ident = keep.tile([P, P], F32, name="ident")
+        make_identity(nc, ident[:])
+        ctx.enter_context(tc.manual_schedule())
+
+        x_raw = {}
+        y_in = {}
+
+        def load(first, count):
+            xt = keep.tile([P, count, 2, DIM], U8, name="x_raw%d" % first, align_bytes=64)
+            yt = keep.tile([P, count, 2, DIM], BF16, name="y%d" % first, align_bytes=64)
+            nc.sync.dma_start(
+                out=xt[:].rearrange("p c b k -> p (c b) k"),
+                in_=x_rows[:, 2 * first : 2 * (first + count), :],
+            )
+            nc.sync.dma_start(
+                out=yt[:].rearrange("p c b k -> p (c b) k"),
+                in_=y_rows[:, 2 * first : 2 * (first + count), :],
+            )
+            for c in range(count):
+                x_raw[first + c] = xt[:, c]
+                y_in[first + c] = yt[:, c]
+
+        x0 = keep.tile([P, 2, DIM], U8, name="x_first", align_bytes=64)
+        nc.sync.dma_start(out=x0[:], in_=x_rows[:, 0:2, :])
+        x_raw[0] = x0[:]
+        sc = keep.tile([P, 2, DIM], F32, name="sc")
+        nc.sync.dma_start(
+            out=sc[:, 0, :], in_=x_scale.rearrange("a b k -> (a b k)").partition_broadcast(P)
+        )
+        wg, wgs = load_weight(nc, keep, wg_words, wg_scales, "wg")
+        x1 = keep.tile([P, 2, DIM], U8, name="x_second", align_bytes=64)
+        nc.sync.dma_start(out=x1[:], in_=x_rows[:, 2:4, :])
+        x_raw[1] = x1[:]
+        y01 = keep.tile([P, 2, 2, DIM], BF16, name="y_first", align_bytes=64)
+        nc.sync.dma_start(out=y01[:].rearrange("p c b k -> p (c b) k"), in_=y_rows[:, 0:4, :])
+        y_in[0] = y01[:, 0]
+        y_in[1] = y01[:, 1]
+        wo, wos = load_weight(nc, keep, wo_words, wo_scales, "wo")
+        for first in range(2, AHEAD, 2):
+            load(first, 2)
+        nc.scalar.copy(out=sc[:, 1, :], in_=sc[:, 0, :])
+
+        xs, x_ps, xg, xc, xcs = {}, {}, {}, {}, {}
+        g_ps, h, h_ps, hg, hc, hcs = {}, {}, {}, {}, {}, {}
+
+        xw = {}
+
+        def widen_x(i):
+            xw[i] = pool.tile([P, SHARE], BF16, name="xw", align_bytes=64)
+            raw = x_raw[i].rearrange("p b k -> p (b k)").bitcast(FP8)
+            nc.scalar.copy(out=xw[i][:], in_=raw[:, 2 * DIM - SHARE :])
+
+        def scale_x(i):
+            split = 2 * DIM - SHARE if i >= 2 else 2 * DIM
+            end = min(split + HINGE, 2 * DIM)
+            xs[i] = pool.tile([P, 2, DIM], BF16, name="xs", bufs=4, align_bytes=64)
+            flat = xs[i][:].rearrange("p b k -> p (b k)")
+            raw = x_raw[i].rearrange("p b k -> p (b k)").bitcast(FP8)
+            scales = sc[:].rearrange("p b k -> p (b k)")
+            nc.vector.tensor_tensor(
+                out=flat[:, :end], in0=raw[:, :end], in1=scales[:, :end], op=ALU.mult
+            )
+            if i >= 2:
+                nc.gpsimd.tensor_tensor(
+                    out=flat[:, split:], in0=xw[i][:], in1=scales[:, split:], op=ALU.mult
+                )
+
+        def turn(ps, src, b):
+            words = src[:].rearrange("p b k -> p (b k)").bitcast(F32)
+            for u in range(2):
+                nc.tensor.transpose(
+                    ps[:, b, u, :], words[:, 256 * b + u : 256 * (b + 1) : 2], ident[:]
+                )
+
+        def empty(grouped, ps):
+            nc.scalar.copy(
+                out=grouped[:].bitcast(F32).rearrange("p (b r u) -> p b r u", b=2, u=2),
+                in_=ps[:].rearrange("p b u r -> p b r u"),
+            )
+
+        def multiply(ps, codes, scales, b, w, ws):
+            cols = slice(P * b, P * (b + 1))
+            nc.tensor.matmul_mx(
+                out=ps[:],
+                lhsT=codes[:, cols].bitcast(FP8X4),
+                lhsT_scale=scales[:, cols],
+                rhs=w[:].bitcast(FP4X4),
+                rhs_scale=ws[:],
+                start=True,
+                stop=True,
+            )
+
+        for j in range(-LEAD, PAIRS + 1):
+            nxt = j + AHEAD
+            if j >= 0 and nxt < PAIRS and nxt % 2 == 0:
+                load(nxt, 2)
+            if 2 <= j + LEAD < PAIRS:
+                widen_x(j + LEAD)
+            if 0 <= j < PAIRS:
+                h[j] = pool.tile([P, 2, DIM], BF16, name="h", align_bytes=64)
+                for b in range(2):
+                    nc.vector.scalar_tensor_tensor(
+                        out=h[j][:, b, :],
+                        in0=g_ps[j, b][:],
+                        scalar=0.0,
+                        in1=y_in[j][:, b, :],
+                        op0=ALU.max,
+                        op1=ALU.mult,
+                    )
+            if 0 <= j + 2 < PAIRS:
+                i = j + 2
+                x_ps[i] = psum.tile([P, 2, 2, P], F32, name="x_ps")
+                for b in range(2):
+                    turn(x_ps[i], xs[i], b)
+                xg[i] = pool.tile([P, 8 * P], BF16, name="xg", align_bytes=64)
+                empty(xg[i], x_ps[i])
+            if 0 <= j < PAIRS:
+                h_ps[j] = psum.tile([P, 2, 2, P], F32, name="h_ps")
+                for b in range(2):
+                    turn(h_ps[j], h[j], b)
+                hg[j] = pool.tile([P, 8 * P], BF16, name="hg", align_bytes=64)
+                empty(hg[j], h_ps[j])
+            if 0 <= j + 1 < PAIRS:
+                i = j + 1
+                xc[i] = pool.tile([P, 2 * P], U32, name="xc", align_bytes=64)
+                xcs[i] = pool.tile([P, 2 * P], U8, name="xcs", align_bytes=64)
+                nc.vector.quantize_mx(out=xc[i][:].bitcast(FP8X4), scales=xcs[i][:], in_=xg[i][:])
+                for b in range(2):
+                    g_ps[i, b] = psum.tile([P, DIM], F32, name="g_ps")
+                    multiply(g_ps[i, b], xc[i], xcs[i], b, wg, wgs)
+            if 0 <= j - 1 < PAIRS:
+                i = j - 1
+                hc[i] = pool.tile([P, 2 * P], U32, name="hc", align_bytes=64)
+                hcs[i] = pool.tile([P, 2 * P], U8, name="hcs", align_bytes=64)
+                nc.vector.quantize_mx(out=hc[i][:].bitcast(FP8X4), scales=hcs[i][:], in_=hg[i][:])
+                o = outs.tile([P, 2, DIM], F32, name="o")
+                for b in range(2):
+                    o_ps = psum.tile([P, DIM], F32, name="o_ps")
+                    multiply(o_ps, hc[i], hcs[i], b, wo, wos)
+                    nc.scalar.copy(out=o[:, b, :], in_=o_ps[:])
+                nc.sync.dma_start(out=o_rows[:, 2 * i : 2 * i + 2, :], in_=o[:])
+            if 0 <= j + LEAD < PAIRS:
+                scale_x(j + LEAD)

@@ -24,6 +24,7 @@ AHEAD = 8
 LEAD = 4
 SHARE = 384
 HINGE = 16
+LAST = PAIRS - 1
 
 
 def load_weight(nc, keep, words, scales, name):
@@ -75,30 +76,31 @@ def tile_multiscaleretention_pb_t_w4_kernel(
                 x_raw[first + c] = xt[:, c]
                 y_in[first + c] = yt[:, c]
 
-        x0 = keep.tile([P, 2, DIM], U8, name="x_first", align_bytes=64)
-        nc.sync.dma_start(out=x0[:], in_=x_rows[:, 0:2, :])
-        x_raw[0] = x0[:]
         sc = keep.tile([P, 2, DIM], F32, name="sc")
         nc.sync.dma_start(
             out=sc[:, 0, :], in_=x_scale.rearrange("a b k -> (a b k)").partition_broadcast(P)
         )
+        x0 = keep.tile([P, 2, DIM], U8, name="x_first", align_bytes=64)
+        nc.sync.dma_start(out=x0[:], in_=x_rows[:, 0:2, :])
+        x_raw[0] = x0[:]
         wg, wgs = load_weight(nc, keep, wg_words, wg_scales, "wg")
-        x1 = keep.tile([P, 2, DIM], U8, name="x_second", align_bytes=64)
-        nc.sync.dma_start(out=x1[:], in_=x_rows[:, 2:4, :])
-        x_raw[1] = x1[:]
+        x1 = keep.tile([P, 3, 2, DIM], U8, name="x_second", align_bytes=64)
+        nc.sync.dma_start(out=x1[:].rearrange("p c b k -> p (c b) k"), in_=x_rows[:, 2:8, :])
         y01 = keep.tile([P, 2, 2, DIM], BF16, name="y_first", align_bytes=64)
-        nc.sync.dma_start(out=y01[:].rearrange("p c b k -> p (c b) k"), in_=y_rows[:, 0:4, :])
-        y_in[0] = y01[:, 0]
-        y_in[1] = y01[:, 1]
+        nc.gpsimd.dma_start(out=y01[:].rearrange("p c b k -> p (c b) k"), in_=y_rows[:, 0:4, :])
+        y23 = keep.tile([P, 2, 2, DIM], BF16, name="y_second", align_bytes=64)
+        nc.sync.dma_start(out=y23[:].rearrange("p c b k -> p (c b) k"), in_=y_rows[:, 4:8, :])
+        for c in range(3):
+            x_raw[1 + c] = x1[:, c]
+        for c in range(2):
+            y_in[c] = y01[:, c]
+            y_in[2 + c] = y23[:, c]
         wo, wos = load_weight(nc, keep, wo_words, wo_scales, "wo")
-        for first in range(2, AHEAD, 2):
+        for first in range(4, AHEAD, 2):
             load(first, 2)
         nc.scalar.copy(out=sc[:, 1, :], in_=sc[:, 0, :])
 
-        xs, x_ps, xg, xc, xcs = {}, {}, {}, {}, {}
-        g_ps, h, h_ps, hg, hc, hcs = {}, {}, {}, {}, {}, {}
-
-        xw = {}
+        xs, x_ps, xw, g_ps, h, h_ps, x_codes, h_codes = {}, {}, {}, {}, {}, {}, {}, {}
 
         def widen_x(i):
             xw[i] = pool.tile([P, SHARE], BF16, name="xw", align_bytes=64)
@@ -106,16 +108,23 @@ def tile_multiscaleretention_pb_t_w4_kernel(
             nc.scalar.copy(out=xw[i][:], in_=raw[:, 2 * DIM - SHARE :])
 
         def scale_x(i):
-            split = 2 * DIM - SHARE if i >= 2 else 2 * DIM
-            end = min(split + HINGE, 2 * DIM)
             xs[i] = pool.tile([P, 2, DIM], BF16, name="xs", bufs=4, align_bytes=64)
             flat = xs[i][:].rearrange("p b k -> p (b k)")
             raw = x_raw[i].rearrange("p b k -> p (b k)").bitcast(FP8)
             scales = sc[:].rearrange("p b k -> p (b k)")
+            if i == 0:
+                for b in range(2):
+                    cols = slice(DIM * b, DIM * (b + 1))
+                    nc.vector.tensor_tensor(
+                        out=flat[:, cols], in0=raw[:, cols], in1=sc[:, 0, :], op=ALU.mult
+                    )
+                return
+            split = 2 * DIM - SHARE if i >= 2 else 2 * DIM
+            end = min(split + HINGE, 2 * DIM)
             nc.vector.tensor_tensor(
                 out=flat[:, :end], in0=raw[:, :end], in1=scales[:, :end], op=ALU.mult
             )
-            if i >= 2:
+            if split < 2 * DIM:
                 nc.gpsimd.tensor_tensor(
                     out=flat[:, split:], in0=xw[i][:], in1=scales[:, split:], op=ALU.mult
                 )
@@ -127,14 +136,15 @@ def tile_multiscaleretention_pb_t_w4_kernel(
                     ps[:, b, u, :], words[:, 256 * b + u : 256 * (b + 1) : 2], ident[:]
                 )
 
-        def empty(grouped, ps):
-            nc.scalar.copy(
-                out=grouped[:].bitcast(F32).rearrange("p (b r u) -> p b r u", b=2, u=2),
-                in_=ps[:].rearrange("p b u r -> p b r u"),
+        def empty(copy, grouped, ps, bs):
+            copy(
+                out=grouped.bitcast(F32).rearrange("p (b r u) -> p b r u", b=2, u=2)[:, bs],
+                in_=ps[:].rearrange("p b u r -> p b r u")[:, bs],
             )
 
-        def multiply(ps, codes, scales, b, w, ws):
-            cols = slice(P * b, P * (b + 1))
+        def multiply(ps, operand, b, w, ws):
+            codes, scales, first = operand
+            cols = slice(first + P * b, first + P * (b + 1))
             nc.tensor.matmul_mx(
                 out=ps[:],
                 lhsT=codes[:, cols].bitcast(FP8X4),
@@ -145,54 +155,80 @@ def tile_multiscaleretention_pb_t_w4_kernel(
                 stop=True,
             )
 
-        for j in range(-LEAD, PAIRS + 1):
+        def relu_times_y(j):
+            h[j] = pool.tile([P, 2, DIM], BF16, name="h", align_bytes=64)
+            for b in range(2):
+                nc.vector.scalar_tensor_tensor(
+                    out=h[j][:, b, :],
+                    in0=g_ps[j, b][:],
+                    scalar=0.0,
+                    in1=y_in[j][:, b, :],
+                    op0=ALU.max,
+                    op1=ALU.mult,
+                )
+
+        for j in range(-LEAD, PAIRS + 2):
             nxt = j + AHEAD
             if j >= 0 and nxt < PAIRS and nxt % 2 == 0:
                 load(nxt, 2)
-            if 2 <= j + LEAD < PAIRS:
-                widen_x(j + LEAD)
             if 0 <= j < PAIRS:
-                h[j] = pool.tile([P, 2, DIM], BF16, name="h", align_bytes=64)
-                for b in range(2):
-                    nc.vector.scalar_tensor_tensor(
-                        out=h[j][:, b, :],
-                        in0=g_ps[j, b][:],
-                        scalar=0.0,
-                        in1=y_in[j][:, b, :],
-                        op0=ALU.max,
-                        op1=ALU.mult,
-                    )
+                relu_times_y(j)
+            grouped = pool.tile([P, 2, 8 * P], BF16, name="grouped", bufs=4, align_bytes=64)
             if 0 <= j + 2 < PAIRS:
                 i = j + 2
                 x_ps[i] = psum.tile([P, 2, 2, P], F32, name="x_ps")
                 for b in range(2):
                     turn(x_ps[i], xs[i], b)
-                xg[i] = pool.tile([P, 8 * P], BF16, name="xg", align_bytes=64)
-                empty(xg[i], x_ps[i])
-            if 0 <= j < PAIRS:
-                h_ps[j] = psum.tile([P, 2, 2, P], F32, name="h_ps")
-                for b in range(2):
-                    turn(h_ps[j], h[j], b)
-                hg[j] = pool.tile([P, 8 * P], BF16, name="hg", align_bytes=64)
-                empty(hg[j], h_ps[j])
-            if 0 <= j + 1 < PAIRS:
-                i = j + 1
-                xc[i] = pool.tile([P, 2 * P], U32, name="xc", align_bytes=64)
-                xcs[i] = pool.tile([P, 2 * P], U8, name="xcs", align_bytes=64)
-                nc.vector.quantize_mx(out=xc[i][:].bitcast(FP8X4), scales=xcs[i][:], in_=xg[i][:])
-                for b in range(2):
-                    g_ps[i, b] = psum.tile([P, DIM], F32, name="g_ps")
-                    multiply(g_ps[i, b], xc[i], xcs[i], b, wg, wgs)
+                    if i == 0:
+                        empty(nc.scalar.copy, grouped[:, 1], x_ps[i], slice(b, b + 1))
+                if i != 0:
+                    empty(nc.scalar.copy, grouped[:, 1], x_ps[i], slice(0, 2))
             if 0 <= j - 1 < PAIRS:
                 i = j - 1
-                hc[i] = pool.tile([P, 2 * P], U32, name="hc", align_bytes=64)
-                hcs[i] = pool.tile([P, 2 * P], U8, name="hcs", align_bytes=64)
-                nc.vector.quantize_mx(out=hc[i][:].bitcast(FP8X4), scales=hcs[i][:], in_=hg[i][:])
+                h_ps[i] = psum.tile([P, 2, 2, P], F32, name="h_ps")
+                for b in range(2):
+                    turn(h_ps[i], h[i], b)
+                    if i == LAST:
+                        copy = nc.vector.tensor_copy if b else nc.scalar.copy
+                        empty(copy, grouped[:, 0], h_ps[i], slice(b, b + 1))
+                if i != LAST:
+                    empty(nc.scalar.copy, grouped[:, 0], h_ps[i], slice(0, 2))
+            if 0 <= j - 2 < PAIRS:
+                i = j - 2
                 o = outs.tile([P, 2, DIM], F32, name="o")
                 for b in range(2):
                     o_ps = psum.tile([P, DIM], F32, name="o_ps")
-                    multiply(o_ps, hc[i], hcs[i], b, wo, wos)
-                    nc.scalar.copy(out=o[:, b, :], in_=o_ps[:])
-                nc.sync.dma_start(out=o_rows[:, 2 * i : 2 * i + 2, :], in_=o[:])
-            if 0 <= j + LEAD < PAIRS:
+                    multiply(o_ps, h_codes[i], b, wo, wos)
+                    copy = nc.vector.tensor_copy if b and i > LAST - 3 else nc.scalar.copy
+                    copy(out=o[:, b, :], in_=o_ps[:])
+                    if i == LAST:
+                        nc.sync.dma_start(out=o_rows[:, 2 * i + b, :], in_=o[:, b, :])
+                if i != LAST:
+                    nc.sync.dma_start(out=o_rows[:, 2 * i : 2 * i + 2, :], in_=o[:])
+            if j >= 0 and j + LEAD < PAIRS:
                 scale_x(j + LEAD)
+            codes = pool.tile([P, 4 * P], U32, name="codes", bufs=4, align_bytes=64)
+            scales = pool.tile([P, 4 * P], U8, name="scales", bufs=4, align_bytes=64)
+            first = 0 if 0 <= j - 1 < PAIRS else 2
+            last = 4 if 0 <= j + 2 < PAIRS else 2
+            parts = [(first, last)]
+            if j + 2 == 0 or j - 1 == LAST:
+                parts = [(first, first + 1), (first + 1, last)]
+            for lo, hi in parts:
+                if lo < hi:
+                    nc.vector.quantize_mx(
+                        out=codes[:, P * lo : P * hi].bitcast(FP8X4),
+                        scales=scales[:, P * lo : P * hi],
+                        in_=grouped[:].rearrange("p s k -> p (s k)")[:, 4 * P * lo : 4 * P * hi],
+                    )
+            h_codes[j - 1] = (codes, scales, 0)
+            x_codes[j + 2] = (codes, scales, 2 * P)
+            if j < 0 and j + LEAD < PAIRS:
+                scale_x(j + LEAD)
+            if 0 <= j + 1 < PAIRS:
+                i = j + 1
+                for b in range(2):
+                    g_ps[i, b] = psum.tile([P, DIM], F32, name="g_ps")
+                    multiply(g_ps[i, b], x_codes[i], b, wg, wgs)
+            if 2 <= j + LEAD + 1 < PAIRS:
+                widen_x(j + LEAD + 1)

@@ -22,7 +22,7 @@ ROWS = TOKENS // P
 PAIRS = ROWS // 2
 AHEAD = 8
 LEAD = 4
-SHARE = 384
+SHARE = 448
 HINGE = 16
 LAST = PAIRS - 1
 
@@ -129,12 +129,18 @@ def tile_multiscaleretention_pb_t_w4_kernel(
                     out=flat[:, split:], in0=xw[i][:], in1=scales[:, split:], op=ALU.mult
                 )
 
-        def turn(ps, src, b):
+        def turn_x(ps, src, b):
             words = src[:].rearrange("p b k -> p (b k)").bitcast(F32)
             for u in range(2):
                 nc.tensor.transpose(
                     ps[:, b, u, :], words[:, 256 * b + u : 256 * (b + 1) : 2], ident[:]
                 )
+
+        def turn_h(ps, src, b):
+            words = src[:].rearrange("p b u c -> p (b u c)").bitcast(F32)
+            for u in range(2):
+                lo = 256 * b + 128 * u
+                nc.tensor.transpose(ps[:, b, u, :], words[:, lo : lo + 128], ident[:])
 
         def empty(copy, grouped, ps, bs):
             copy(
@@ -156,43 +162,49 @@ def tile_multiscaleretention_pb_t_w4_kernel(
             )
 
         def relu_times_y(j):
-            h[j] = pool.tile([P, 2, DIM], BF16, name="h", align_bytes=64)
+            h[j] = pool.tile([P, 2, 2, DIM // 2], BF16, name="h", align_bytes=64)
             for b in range(2):
-                nc.vector.scalar_tensor_tensor(
-                    out=h[j][:, b, :],
-                    in0=g_ps[j, b][:],
-                    scalar=0.0,
-                    in1=y_in[j][:, b, :],
-                    op0=ALU.max,
-                    op1=ALU.mult,
-                )
+                g_pairs = g_ps[j, b][:].rearrange("p (q u e) -> p q u e", u=2, e=2)
+                y_pairs = y_in[j][:, b, :].rearrange("p (q u e) -> p q u e", u=2, e=2)
+                for u in range(2):
+                    nc.vector.scalar_tensor_tensor(
+                        out=h[j][:, b, u, :].rearrange("p (q e) -> p q e", e=2),
+                        in0=g_pairs[:, :, u, :],
+                        scalar=0.0,
+                        in1=y_pairs[:, :, u, :],
+                        op0=ALU.max,
+                        op1=ALU.mult,
+                    )
 
+        grouped = {}
         for j in range(-LEAD, PAIRS + 2):
             nxt = j + AHEAD
             if j >= 0 and nxt < PAIRS and nxt % 2 == 0:
                 load(nxt, 2)
             if 0 <= j < PAIRS:
                 relu_times_y(j)
-            grouped = pool.tile([P, 2, 8 * P], BF16, name="grouped", bufs=4, align_bytes=64)
-            if 0 <= j + 2 < PAIRS:
-                i = j + 2
-                x_ps[i] = psum.tile([P, 2, 2, P], F32, name="x_ps")
-                for b in range(2):
-                    turn(x_ps[i], xs[i], b)
-                    if i == 0:
-                        empty(nc.scalar.copy, grouped[:, 1], x_ps[i], slice(b, b + 1))
-                if i != 0:
-                    empty(nc.scalar.copy, grouped[:, 1], x_ps[i], slice(0, 2))
-            if 0 <= j - 1 < PAIRS:
-                i = j - 1
-                h_ps[i] = psum.tile([P, 2, 2, P], F32, name="h_ps")
-                for b in range(2):
-                    turn(h_ps[i], h[i], b)
-                    if i == LAST:
-                        copy = nc.vector.tensor_copy if b else nc.scalar.copy
-                        empty(copy, grouped[:, 0], h_ps[i], slice(b, b + 1))
-                if i != LAST:
-                    empty(nc.scalar.copy, grouped[:, 0], h_ps[i], slice(0, 2))
+            if 2 <= j + LEAD < PAIRS:
+                widen_x(j + LEAD)
+            if j >= 0 and j + LEAD < PAIRS:
+                scale_x(j + LEAD)
+            first = 0 if 0 <= j - 1 < PAIRS else 2
+            last = 4 if 0 <= j + 2 < PAIRS else 2
+            if first < last:
+                codes = pool.tile([P, 4 * P], U32, name="codes", bufs=4, align_bytes=64)
+                scales = pool.tile([P, 4 * P], U8, name="scales", bufs=4, align_bytes=64)
+                parts = [(first, last)]
+                if j + 2 == 0 or j - 1 == LAST:
+                    parts = [(first, first + 1), (first + 1, last)]
+                for lo, hi in parts:
+                    nc.vector.quantize_mx(
+                        out=codes[:, P * lo : P * hi].bitcast(FP8X4),
+                        scales=scales[:, P * lo : P * hi],
+                        in_=grouped[j][:].rearrange("p s k -> p (s k)")[:, 4 * P * lo : 4 * P * hi],
+                    )
+                h_codes[j - 1] = (codes, scales, 0)
+                x_codes[j + 2] = (codes, scales, 2 * P)
+            if j < 0 and j + LEAD < PAIRS:
+                scale_x(j + LEAD)
             if 0 <= j - 2 < PAIRS:
                 i = j - 2
                 o = outs.tile([P, 2, DIM], F32, name="o")
@@ -205,30 +217,29 @@ def tile_multiscaleretention_pb_t_w4_kernel(
                         nc.sync.dma_start(out=o_rows[:, 2 * i + b, :], in_=o[:, b, :])
                 if i != LAST:
                     nc.sync.dma_start(out=o_rows[:, 2 * i : 2 * i + 2, :], in_=o[:])
-            if j >= 0 and j + LEAD < PAIRS:
-                scale_x(j + LEAD)
-            codes = pool.tile([P, 4 * P], U32, name="codes", bufs=4, align_bytes=64)
-            scales = pool.tile([P, 4 * P], U8, name="scales", bufs=4, align_bytes=64)
-            first = 0 if 0 <= j - 1 < PAIRS else 2
-            last = 4 if 0 <= j + 2 < PAIRS else 2
-            parts = [(first, last)]
-            if j + 2 == 0 or j - 1 == LAST:
-                parts = [(first, first + 1), (first + 1, last)]
-            for lo, hi in parts:
-                if lo < hi:
-                    nc.vector.quantize_mx(
-                        out=codes[:, P * lo : P * hi].bitcast(FP8X4),
-                        scales=scales[:, P * lo : P * hi],
-                        in_=grouped[:].rearrange("p s k -> p (s k)")[:, 4 * P * lo : 4 * P * hi],
-                    )
-            h_codes[j - 1] = (codes, scales, 0)
-            x_codes[j + 2] = (codes, scales, 2 * P)
-            if j < 0 and j + LEAD < PAIRS:
-                scale_x(j + LEAD)
             if 0 <= j + 1 < PAIRS:
                 i = j + 1
                 for b in range(2):
                     g_ps[i, b] = psum.tile([P, DIM], F32, name="g_ps")
                     multiply(g_ps[i, b], x_codes[i], b, wg, wgs)
-            if 2 <= j + LEAD + 1 < PAIRS:
-                widen_x(j + LEAD + 1)
+            if -3 <= j < PAIRS:
+                grouped[j + 1] = pool.tile([P, 2, 8 * P], BF16, name="grouped", align_bytes=64)
+            if 0 <= j < PAIRS:
+                i = j
+                h_ps[i] = psum.tile([P, 2, 2, P], F32, name="h_ps")
+                for b in range(2):
+                    turn_h(h_ps[i], h[i], b)
+                    if i == LAST:
+                        copy = nc.vector.tensor_copy if b else nc.scalar.copy
+                        empty(copy, grouped[j + 1][:, 0], h_ps[i], slice(b, b + 1))
+                if i != LAST:
+                    empty(nc.scalar.copy, grouped[j + 1][:, 0], h_ps[i], slice(0, 2))
+            if 0 <= j + 3 < PAIRS:
+                i = j + 3
+                x_ps[i] = psum.tile([P, 2, 2, P], F32, name="x_ps")
+                for b in range(2):
+                    turn_x(x_ps[i], xs[i], b)
+                    if i == 0:
+                        empty(nc.scalar.copy, grouped[j + 1][:, 1], x_ps[i], slice(b, b + 1))
+                if i != 0:
+                    empty(nc.scalar.copy, grouped[j + 1][:, 1], x_ps[i], slice(0, 2))

@@ -22,7 +22,7 @@ ROWS = TOKENS // P
 PAIRS = ROWS // 2
 AHEAD = 8
 LEAD = 4
-SHARE = 448
+SHARE = 416
 HINGE = 16
 LAST = PAIRS - 1
 
@@ -51,7 +51,7 @@ def tile_multiscaleretention_pb_t_w4_kernel(
     with ExitStack() as ctx:
         keep = ctx.enter_context(tc.tile_pool(name="keep", bufs=1))
         pool = ctx.enter_context(tc.tile_pool(name="pool", bufs=3))
-        outs = ctx.enter_context(tc.tile_pool(name="outs", bufs=4))
+        outs = ctx.enter_context(tc.tile_pool(name="outs", bufs=20))
         psum = ctx.enter_context(tc.psum_pool(name="psum", bufs=2))
 
         ident = keep.tile([P, P], F32, name="ident")
@@ -96,8 +96,8 @@ def tile_multiscaleretention_pb_t_w4_kernel(
             y_in[c] = y01[:, c]
             y_in[2 + c] = y23[:, c]
         wo, wos = load_weight(nc, keep, wo_words, wo_scales, "wo")
-        for first in range(4, AHEAD, 2):
-            load(first, 2)
+        for first in range(4, AHEAD, 4):
+            load(first, 4)
         nc.scalar.copy(out=sc[:, 1, :], in_=sc[:, 0, :])
 
         xs, x_ps, xw, g_ps, h, h_ps, x_codes, h_codes = {}, {}, {}, {}, {}, {}, {}, {}
@@ -119,7 +119,7 @@ def tile_multiscaleretention_pb_t_w4_kernel(
                         out=flat[:, cols], in0=raw[:, cols], in1=sc[:, 0, :], op=ALU.mult
                     )
                 return
-            split = 2 * DIM - SHARE if i >= 2 else 2 * DIM
+            split = 2 * DIM - SHARE if i >= 3 else 2 * DIM
             end = min(split + HINGE, 2 * DIM)
             nc.vector.tensor_tensor(
                 out=flat[:, :end], in0=raw[:, :end], in1=scales[:, :end], op=ALU.mult
@@ -179,11 +179,11 @@ def tile_multiscaleretention_pb_t_w4_kernel(
         grouped = {}
         for j in range(-LEAD, PAIRS + 2):
             nxt = j + AHEAD
-            if j >= 0 and nxt < PAIRS and nxt % 2 == 0:
-                load(nxt, 2)
+            if j >= 0 and nxt < PAIRS and nxt % 4 == 0:
+                load(nxt, 4)
             if 0 <= j < PAIRS:
                 relu_times_y(j)
-            if 2 <= j + LEAD < PAIRS:
+            if 3 <= j + LEAD < PAIRS:
                 widen_x(j + LEAD)
             if j >= 0 and j + LEAD < PAIRS:
                 scale_x(j + LEAD)

from contextlib import ExitStack

import concourse.mybir as mybir
from concourse.masks import make_identity

F32 = mybir.dt.float32
BF16 = mybir.dt.bfloat16
I32 = mybir.dt.int32
U32 = mybir.dt.uint32
U8 = mybir.dt.uint8
FP8 = mybir.dt.float8_e4m3fn
FP8X4 = mybir.dt.float8_e4m3fn_x4
FP4X4 = mybir.dt.float4_e2m1fn_x4
ALU = mybir.AluOpType

P = 128
TOKENS = 8192
DIM = 512
FLOPS = 2 * 2 * TOKENS * DIM * DIM

ROWS = TOKENS // P
PAIRS = ROWS // 2
AHEAD = 8
LEAD = 4
SHARE = 416
HINGE = 16
LAST = PAIRS - 1


def load_weight(nc, keep, words, scales, name):
    w = keep.tile([P, 2 * DIM], U8, name=name + "_codes", align_bytes=64)
    s = keep.tile([P, DIM], U8, name=name + "_scales", align_bytes=64)
    nc.vector.memset(s[:].bitcast(I32), 0)
    nc.sync.dma_start(out=w[:], in_=words[0])
    for q in range(4):
        nc.sync.dma_start(
            out=s[32 * q : 32 * q + 4, :].bitcast(I32),
            in_=scales[0][4 * q : 4 * q + 4, :].bitcast(I32),
        )
    return w, s


def tile_multiscaleretention_pb_t_w4_kernel(
    tc, x_bytes, x_scale, y_norm, wg_words, wg_scales, wo_words, wo_scales, out
):
    nc = tc.nc
    x_rows = x_bytes.rearrange("b s k -> (b s) k").rearrange("(p r) k -> p r k", p=P)
    y_rows = y_norm.rearrange("b s k -> (b s) k").rearrange("(p r) k -> p r k", p=P)
    o_rows = out.rearrange("b s k -> (b s) k").rearrange("(p r) k -> p r k", p=P)

    with ExitStack() as ctx:
        keep = ctx.enter_context(tc.tile_pool(name="keep", bufs=1))
        pool = ctx.enter_context(tc.tile_pool(name="pool", bufs=3))
        outs = ctx.enter_context(tc.tile_pool(name="outs", bufs=20))
        psum = ctx.enter_context(tc.psum_pool(name="psum", bufs=2))

        ident = keep.tile([P, P], F32, name="ident")
        make_identity(nc, ident[:])
        ctx.enter_context(tc.manual_schedule())

        x_raw = {}
        y_in = {}

        def load(first, count):
            xt = keep.tile([P, count, 2, DIM], U8, name="x_raw%d" % first, align_bytes=64)
            yt = keep.tile([P, count, 2, DIM], BF16, name="y%d" % first, align_bytes=64)
            nc.sync.dma_start(
                out=xt[:].rearrange("p c b k -> p (c b) k"),
                in_=x_rows[:, 2 * first : 2 * (first + count), :],
            )
            nc.sync.dma_start(
                out=yt[:].rearrange("p c b k -> p (c b) k"),
                in_=y_rows[:, 2 * first : 2 * (first + count), :],
            )
            for c in range(count):
                x_raw[first + c] = xt[:, c]
                y_in[first + c] = yt[:, c]

        sc = keep.tile([P, 2, DIM], F32, name="sc")
        nc.sync.dma_start(
            out=sc[:, 0, :], in_=x_scale.rearrange("a b k -> (a b k)").partition_broadcast(P)
        )
        x0 = keep.tile([P, 2, DIM], U8, name="x_first", align_bytes=64)
        nc.sync.dma_start(out=x0[:], in_=x_rows[:, 0:2, :])
        x_raw[0] = x0[:]
        wg, wgs = load_weight(nc, keep, wg_words, wg_scales, "wg")
        x1 = keep.tile([P, 3, 2, DIM], U8, name="x_second", align_bytes=64)
        nc.sync.dma_start(out=x1[:].rearrange("p c b k -> p (c b) k"), in_=x_rows[:, 2:8, :])
        y01 = keep.tile([P, 2, 2, DIM], BF16, name="y_first", align_bytes=64)
        nc.gpsimd.dma_start(out=y01[:].rearrange("p c b k -> p (c b) k"), in_=y_rows[:, 0:4, :])
        y23 = keep.tile([P, 2, 2, DIM], BF16, name="y_second", align_bytes=64)
        nc.sync.dma_start(out=y23[:].rearrange("p c b k -> p (c b) k"), in_=y_rows[:, 4:8, :])
        for c in range(3):
            x_raw[1 + c] = x1[:, c]
        for c in range(2):
            y_in[c] = y01[:, c]
            y_in[2 + c] = y23[:, c]
        wo, wos = load_weight(nc, keep, wo_words, wo_scales, "wo")
        for first in range(4, AHEAD, 4):
            load(first, 4)
        nc.scalar.copy(out=sc[:, 1, :], in_=sc[:, 0, :])

        xs, x_ps, xw, g_ps, h, h_ps, x_codes, h_codes = {}, {}, {}, {}, {}, {}, {}, {}

        def widen_x(i):
            xw[i] = pool.tile([P, SHARE], BF16, name="xw", align_bytes=64)
            raw = x_raw[i].rearrange("p b k -> p (b k)").bitcast(FP8)
            nc.scalar.copy(out=xw[i][:], in_=raw[:, 2 * DIM - SHARE :])

        def scale_x(i):
            xs[i] = pool.tile([P, 2, DIM], BF16, name="xs", bufs=4, align_bytes=64)
            flat = xs[i][:].rearrange("p b k -> p (b k)")
            raw = x_raw[i].rearrange("p b k -> p (b k)").bitcast(FP8)
            scales = sc[:].rearrange("p b k -> p (b k)")
            if i == 0:
                for b in range(2):
                    cols = slice(DIM * b, DIM * (b + 1))
                    nc.vector.tensor_tensor(
                        out=flat[:, cols], in0=raw[:, cols], in1=sc[:, 0, :], op=ALU.mult
                    )
                return
            split = 2 * DIM - SHARE if i >= 3 else 2 * DIM
            end = min(split + HINGE, 2 * DIM)
            nc.vector.tensor_tensor(
                out=flat[:, :end], in0=raw[:, :end], in1=scales[:, :end], op=ALU.mult
            )
            if split < 2 * DIM:
                nc.gpsimd.tensor_tensor(
                    out=flat[:, split:], in0=xw[i][:], in1=scales[:, split:], op=ALU.mult
                )

        def turn_x(ps, src, b):
            words = src[:].rearrange("p b k -> p (b k)").bitcast(F32)
            for u in range(2):
                nc.tensor.transpose(
                    ps[:, b, u, :], words[:, 256 * b + u : 256 * (b + 1) : 2], ident[:]
                )

        def turn_h(ps, src, b):
            words = src[:].rearrange("p b u c -> p (b u c)").bitcast(F32)
            for u in range(2):
                lo = 256 * b + 128 * u
                nc.tensor.transpose(ps[:, b, u, :], words[:, lo : lo + 128], ident[:])

        def empty(copy, grouped, ps, bs):
            copy(
                out=grouped.bitcast(F32).rearrange("p (b r u) -> p b r u", b=2, u=2)[:, bs],
                in_=ps[:].rearrange("p b u r -> p b r u")[:, bs],
            )

        def multiply(ps, operand, b, w, ws):
            codes, scales, first = operand
            cols = slice(first + P * b, first + P * (b + 1))
            nc.tensor.matmul_mx(
                out=ps[:],
                lhsT=codes[:, cols].bitcast(FP8X4),
                lhsT_scale=scales[:, cols],
                rhs=w[:].bitcast(FP4X4),
                rhs_scale=ws[:],
                start=True,
                stop=True,
            )

        def relu_times_y(j):
            h[j] = pool.tile([P, 2, 2, DIM // 2], BF16, name="h", align_bytes=64)
            for b in range(2):
                g_pairs = g_ps[j, b][:].rearrange("p (q u e) -> p q u e", u=2, e=2)
                y_pairs = y_in[j][:, b, :].rearrange("p (q u e) -> p q u e", u=2, e=2)
                for u in range(2):
                    nc.vector.scalar_tensor_tensor(
                        out=h[j][:, b, u, :].rearrange("p (q e) -> p q e", e=2),
                        in0=g_pairs[:, :, u, :],
                        scalar=0.0,
                        in1=y_pairs[:, :, u, :],
                        op0=ALU.max,
                        op1=ALU.mult,
                    )

        grouped = {}
        for j in range(-LEAD, PAIRS + 2):
            nxt = j + AHEAD
            if j >= 0 and nxt < PAIRS and nxt % 4 == 0:
                load(nxt, 4)
            if 0 <= j < PAIRS:
                relu_times_y(j)
            if 3 <= j + LEAD < PAIRS:
                widen_x(j + LEAD)
            if j >= 0 and j + LEAD < PAIRS:
                scale_x(j + LEAD)
            first = 0 if 0 <= j - 1 < PAIRS else 2
            last = 4 if 0 <= j + 2 < PAIRS else 2
            if first < last:
                codes = pool.tile([P, 4 * P], U32, name="codes", bufs=4, align_bytes=64)
                scales = pool.tile([P, 4 * P], U8, name="scales", bufs=4, align_bytes=64)
                parts = [(first, last)]
                if j + 2 == 0 or j - 1 == LAST:
                    parts = [(first, first + 1), (first + 1, last)]
                for lo, hi in parts:
                    nc.vector.quantize_mx(
                        out=codes[:, P * lo : P * hi].bitcast(FP8X4),
                        scales=scales[:, P * lo : P * hi],
                        in_=grouped[j][:].rearrange("p s k -> p (s k)")[:, 4 * P * lo : 4 * P * hi],
                    )
                h_codes[j - 1] = (codes, scales, 0)
                x_codes[j + 2] = (codes, scales, 2 * P)
            if j < 0 and j + LEAD < PAIRS:
                scale_x(j + LEAD)
            if 0 <= j - 2 < PAIRS:
                i = j - 2
                o = outs.tile([P, 2, DIM], F32, name="o")
                for b in range(2):
                    o_ps = psum.tile([P, DIM], F32, name="o_ps")
                    multiply(o_ps, h_codes[i], b, wo, wos)
                    copy = nc.vector.tensor_copy if b and i > LAST - 3 else nc.scalar.copy
                    copy(out=o[:, b, :], in_=o_ps[:])
                    if i == LAST:
                        nc.sync.dma_start(out=o_rows[:, 2 * i + b, :], in_=o[:, b, :])
                if i != LAST:
                    nc.sync.dma_start(out=o_rows[:, 2 * i : 2 * i + 2, :], in_=o[:])
            if 0 <= j + 1 < PAIRS:
                i = j + 1
                for b in range(2):
                    g_ps[i, b] = psum.tile([P, DIM], F32, name="g_ps")
                    multiply(g_ps[i, b], x_codes[i], b, wg, wgs)
            if -3 <= j < PAIRS:
                grouped[j + 1] = pool.tile([P, 2, 8 * P], BF16, name="grouped", align_bytes=64)
            if 0 <= j < PAIRS:
                i = j
                h_ps[i] = psum.tile([P, 2, 2, P], F32, name="h_ps")
                for b in range(2):
                    turn_h(h_ps[i], h[i], b)
                    if i == LAST:
                        copy = nc.vector.tensor_copy if b else nc.scalar.copy
                        empty(copy, grouped[j + 1][:, 0], h_ps[i], slice(b, b + 1))
                if i != LAST:
                    empty(nc.scalar.copy, grouped[j + 1][:, 0], h_ps[i], slice(0, 2))
            if 0 <= j + 3 < PAIRS:
                i = j + 3
                x_ps[i] = psum.tile([P, 2, 2, P], F32, name="x_ps")
                for b in range(2):
                    turn_x(x_ps[i], xs[i], b)
                    if i == 0:
                        empty(nc.scalar.copy, grouped[j + 1][:, 1], x_ps[i], slice(b, b + 1))
                if i != 0:
                    empty(nc.scalar.copy, grouped[j + 1][:, 1], x_ps[i], slice(0, 2))
